import numpy as np
import ml_dtypes


def mxq(x, axis, fmt="e4m3"):
    dtype, down = {"e4m3": (ml_dtypes.float8_e4m3fn, 7), "e5m2": (ml_dtypes.float8_e5m2, 14)}[fmt]
    v = np.moveaxis(np.asarray(x, np.float32).astype(ml_dtypes.bfloat16).astype(np.float64), axis, -1)
    blocks = v.reshape(v.shape[:-1] + (-1, 32))
    amax = np.abs(blocks).max(-1, keepdims=True)
    byte = np.maximum(np.where(amax > 0, np.frexp(amax)[1] - 1 + 127, 0) - down, 1)
    scale = np.exp2(byte - 127.0)
    codes = (blocks / scale).astype(np.float32).astype(dtype).astype(np.float64)
    return np.moveaxis((codes * scale).reshape(v.shape), -1, axis)


WIDE = False


def mx_kscale(k):
    if not WIDE:
        return np.ones(k)
    levels = np.array([10, -10, 5, -5, 0])
    if k % 512:
        return np.exp2(np.random.permutation(np.resize(levels, k // 32))).repeat(32)
    a = np.empty((k // 512, 16))
    for p in range(k // 512):
        a[p, :8] = np.random.permutation(np.resize(levels, 8))
        for g in range(8):
            far = levels[np.abs(levels - a[p, g]) >= 10]
            a[p, g + 8] = far[np.random.randint(len(far))]
    return np.exp2(a.ravel()).repeat(32)


BF16 = ml_dtypes.bfloat16


def bf(x):
    return np.asarray(x, np.float32).astype(BF16)


def f64(x):
    return np.asarray(x).astype(np.float64)


N, H, O, L = 1024, 512, 512, 4


def represent(h):
    n = h.shape[0]
    total = np.sum(h, axis=0, keepdims=True)
    return (n * h - total) / (n - 1)


def sigmoid(v):
    return 1.0 / (1.0 + np.exp(-v))


def setup_inputs():
    t = mx_kscale(H)
    mu = np.random.standard_normal(H)
    return {"h": bf((np.random.standard_normal((N, H)) * 1.2 + mu) * t),
            "w": bf(np.random.standard_normal((H, H)) * 0.6 / np.sqrt(H) * t[:, None] / t[None, :]),
            "w_ff": bf(np.random.standard_normal((O, H)) * 0.6 / np.sqrt(H) / t[None, :]),
            "b_ff": bf(np.random.standard_normal(O) * 0.3)}


def reference(h, w, w_ff, b_ff):
    h = f64(h)
    r = represent(h)
    f = mxq(r, 1, "e4m3") @ mxq(f64(w), 1, "e4m3").T
    h_new = f + h
    return sigmoid((mxq(h_new, 1, "e4m3") @ mxq(f64(w_ff), 1, "e4m3").T) + f64(b_ff))

@@ -1,0 +1,324 @@
+from contextlib import ExitStack
+
+import concourse.mybir as mybir
+from concourse.masks import make_identity
+
+N_ROWS, H, O = 1024, 512, 512
+FLOPS = 2 * N_ROWS * H * H + 2 * N_ROWS * H * O
+
+F32 = mybir.dt.float32
+BF16 = mybir.dt.bfloat16
+U32 = mybir.dt.uint32
+U8 = mybir.dt.uint8
+FP8X4 = mybir.dt.float8_e4m3fn_x4
+ALU = mybir.AluOpType
+ACT = mybir.ActivationFunctionType
+AX = mybir.AxisListType
+
+P = 128
+NT = N_ROWS // P
+BANK1 = F32
+
+
+def tile_differ_amplifier_pa_kernel(tc, h, w, w_ff, b_ff, out):
+    nc = tc.nc
+    with ExitStack() as ctx:
+        const = ctx.enter_context(tc.tile_pool(name="const", bufs=1))
+        keep = ctx.enter_context(tc.tile_pool(name="keep", bufs=1))
+        work = ctx.enter_context(tc.tile_pool(name="work", bufs=8))
+        psum = ctx.enter_context(tc.psum_pool(name="psum", bufs=8))
+        ctx.enter_context(tc.manual_schedule())
+
+        h_v = h.rearrange("(p i) k -> p i k", i=NT)
+        out_v = out.rearrange("(p i) o -> p i o", i=NT)
+        w_v = w.rearrange("(j m) k -> m j k", j=4)
+        wff_v = w_ff.rearrange("(j m) k -> m j k", j=4)
+
+        h_nat = []
+        for j in range(4):
+            t = keep.tile([P, 2, H], BF16, name="h_nat%d" % j)
+            nc.sync.dma_start(out=t[:], in_=h_v[:, 2 * j : 2 * j + 2, :])
+            h_nat.append(t)
+        w_nat = []
+        for b in range(2):
+            t = keep.tile([P, 2, H], BF16, name="w_nat%d" % b)
+            nc.sync.dma_start(out=t[:], in_=w_v[:, 2 * b : 2 * b + 2, :])
+            w_nat.append(t)
+        wff_nat = []
+        for b in range(2):
+            t = keep.tile([P, 2, H], BF16, name="wff_nat%d" % b)
+            nc.sync.dma_start(out=t[:], in_=wff_v[:, 2 * b : 2 * b + 2, :])
+            wff_nat.append(t)
+
+        ones = const.tile([P, P], BF16, name="ones")
+        nc.vector.memset(ones[:], 1.0)
+
+        ident = const.tile([P, P], F32, name="ident")
+        make_identity(nc, ident[:])
+        brow = const.tile([P, O], BF16, name="brow")
+        nc.vector.memset(brow[:], 0.0)
+        nc.scalar.dma_start(out=brow[0:1, :], in_=b_ff.rearrange("(a o) -> a o", a=1))
+        warm = const.tile([P, 1], F32, name="warm")
+        nc.vector.memset(warm[:], 0.0)
+        nc.scalar.activation(out=warm[:], in_=warm[:], func=ACT.Sigmoid)
+
+
+        def transpose_words(bank, src_bf16):
+            words = src_bf16.bitcast(F32)
+            for u in range(2):
+                nc.tensor.transpose(bank[:, u, :], words[:, u : H // 2 : 2], ident[:])
+
+        tot_ps = psum.tile([P, 4, NT], F32, tag="bank", name="tot_ps")
+        hI = [None] * 4
+
+        def totals(j):
+            for ii in range(2):
+                i = 2 * j + ii
+                for t in range(4):
+                    nc.tensor.matmul(
+                        tot_ps[:, t, i : i + 1],
+                        lhsT=h_nat[j][:, ii, t:H:4],
+                        rhs=ones[:, 0:1],
+                        start=True,
+                        stop=True,
+                    )
+
+        tp_h = [None] * 4
+
+        def th(j):
+            tp_h[j] = psum.tile([P, 2, 2, P], F32, tag="bank", name="tp_h")
+            for ii in range(2):
+                transpose_words(tp_h[j][:, ii], h_nat[j][:, ii, :])
+
+        def hi(j):
+            hI[j] = keep.tile([P, 2 * P * 4], BF16, name="hI%d" % j, align_bytes=64)
+            nc.scalar.copy(
+                out=hI[j][:].bitcast(F32).rearrange("p (i n u) -> p i n u", i=2, u=2),
+                in_=tp_h[j][:].rearrange("p i u n -> p i n u"),
+            )
+
+        def weight_tiles(label):
+            grouped = keep.tile([P, O * 4], BF16, name=label + "_I", align_bytes=64)
+            codes = keep.tile([P, O], U32, name=label + "_codes", align_bytes=64)
+            scales = keep.tile([P, O], U8, name=label + "_scales", align_bytes=64)
+            return grouped, codes, scales
+
+        tp_w = {}
+
+        def tw(label, nat, b):
+            tp_w[(label, b)] = psum.tile([P, 2, 2, P], F32, tag="bank", name="tp_w")
+            for jj in range(2):
+                transpose_words(tp_w[(label, b)][:, jj], nat[b][:, jj, :])
+
+        def cw(label, grouped, b):
+            dst = grouped[:, b * 1024 : (b + 1) * 1024].bitcast(F32)
+            nc.scalar.copy(
+                out=dst.rearrange("p (j m u) -> p j m u", j=2, u=2),
+                in_=tp_w[(label, b)][:].rearrange("p j u m -> p j m u"),
+            )
+
+        def quant_weight(grouped, codes, scales, b):
+            nc.vector.quantize_mx(
+                out=codes[:, b * 256 : (b + 1) * 256].bitcast(FP8X4),
+                scales=scales[:, b * 256 : (b + 1) * 256],
+                in_=grouped[:, b * 1024 : (b + 1) * 1024],
+            )
+
+        w_I, w_codes, w_scales = weight_tiles("w")
+        wff_I, wff_codes, wff_scales = weight_tiles("wff")
+        tot = const.tile([P, 4], F32, name="tot")
+        cmean = const.tile([P, 4], F32, name="cmean")
+        biasB = const.tile([P, O], F32, name="biasB")
+
+        rI = []
+        r_codes = []
+        r_scales = []
+        hnI = []
+        hn_codes = []
+        hn_scales = []
+        for half in range(2):
+            rI.append(keep.tile([P, 2048], BF16, name="rI%d" % half, align_bytes=64))
+            r_codes.append(keep.tile([P, 512], U32, name="r_codes%d" % half, align_bytes=64))
+            r_scales.append(keep.tile([P, 512], U8, name="r_scales%d" % half, align_bytes=64))
+            hnI.append(keep.tile([P, 2048], BF16, name="hnI%d" % half, align_bytes=64))
+            hn_codes.append(keep.tile([P, 512], U32, name="hn_codes%d" % half, align_bytes=64))
+            hn_scales.append(keep.tile([P, 512], U8, name="hn_scales%d" % half, align_bytes=64))
+        s1 = [None] * NT
+        hn = [None] * NT
+        tp_hn = [None] * NT
+        s2 = [None] * NT
+        pre = [None] * NT
+
+        def st_a(j):
+            nc.vector.scalar_tensor_tensor(
+                out=rI[j // 2][:, (j % 2) * 1024 : (j % 2 + 1) * 1024].rearrange("p (n t) -> p n t", t=4),
+                in0=hI[j][:].rearrange("p (n t) -> p n t", t=4),
+                scalar=float(N_ROWS) / (N_ROWS - 1),
+                in1=cmean[:].unsqueeze(1).to_broadcast([P, 2 * P, 4]),
+                op0=ALU.mult,
+                op1=ALU.subtract,
+            )
+
+        def st_b(half):
+            nc.vector.quantize_mx(
+                out=r_codes[half][:].bitcast(FP8X4), scales=r_scales[half][:], in_=rI[half][:]
+            )
+
+        def st_c(i):
+            half, q = i // 4, i % 4
+            s1[i] = psum.tile([P, H], BANK1, tag="bank", name="s1")
+            nc.tensor.matmul_mx(
+                out=s1[i][:],
+                lhsT=r_codes[half][:, q * P : (q + 1) * P].bitcast(FP8X4),
+                lhsT_scale=r_scales[half][:, q * P : (q + 1) * P],
+                rhs=w_codes[:].bitcast(FP8X4),
+                rhs_scale=w_scales[:],
+                start=True,
+                stop=True,
+            )
+
+        def st_d(i):
+            hn[i] = work.tile([P, H], BF16, name="hn")
+            nc.vector.tensor_tensor(out=hn[i][:], in0=s1[i][:], in1=h_nat[i // 2][:, i % 2, :], op=ALU.add)
+
+        def st_e(i):
+            tp_hn[i] = psum.tile([P, 2, P], F32, tag="bank", name="tp_hn")
+            transpose_words(tp_hn[i], hn[i][:])
+
+        def st_f(i):
+            half, q = i // 4, i % 4
+            nc.scalar.copy(
+                out=hnI[half][:, q * 512 : (q + 1) * 512].bitcast(F32).rearrange("p (n u) -> p n u", u=2),
+                in_=tp_hn[i][:].rearrange("p u n -> p n u"),
+            )
+
+        def st_g(part):
+            half, lo, hi_ = {0: (0, 0, 4), 1: (1, 0, 4), 8: (1, 0, 2), 9: (1, 2, 4)}[part]
+            nc.vector.quantize_mx(
+                out=hn_codes[half][:, lo * P : hi_ * P].bitcast(FP8X4),
+                scales=hn_scales[half][:, lo * P : hi_ * P],
+                in_=hnI[half][:, lo * 4 * P : hi_ * 4 * P],
+            )
+
+        def st_h(i):
+            half, q = i // 4, i % 4
+            s2[i] = psum.tile([P, O], F32, tag="bank", name="s2")
+            nc.tensor.matmul_mx(
+                out=s2[i][:],
+                lhsT=hn_codes[half][:, q * P : (q + 1) * P].bitcast(FP8X4),
+                lhsT_scale=hn_scales[half][:, q * P : (q + 1) * P],
+                rhs=wff_codes[:].bitcast(FP8X4),
+                rhs_scale=wff_scales[:],
+                start=True,
+                stop=True,
+            )
+
+        res = [None] * NT
+
+        def st_i(i, lo=0, hi_=O):
+            if lo == 0:
+                pre[i] = work.tile([P, O], F32, name="pre")
+            nc.vector.tensor_tensor(out=pre[i][:, lo:hi_], in0=s2[i][:, lo:hi_], in1=biasB[:, lo:hi_], op=ALU.add)
+
+        def st_j(i, lo=0, hi_=O):
+            if lo == 0:
+                res[i] = work.tile([P, O], F32, name="res")
+            nc.scalar.activation(out=res[i][:, lo:hi_], in_=pre[i][:, lo:hi_], func=ACT.Sigmoid)
+            nc.sync.dma_start(out=out_v[:, i, lo:hi_], in_=res[i][:, lo:hi_])
+
+        totals(0)
+        th(0)
+        hi(0)
+        totals(1)
+        totals(2)
+        totals(3)
+        nc.vector.tensor_reduce(out=tot[:], in_=tot_ps[:], axis=AX.X, op=ALU.add)
+        nc.vector.tensor_scalar_mul(cmean[:], tot[:], 1.0 / (N_ROWS - 1))
+        th(1)
+        hi(1)
+        tw("w", w_nat, 0)
+        cw("w", w_I, 0)
+        tw("w", w_nat, 1)
+        cw("w", w_I, 1)
+        th(2)
+        hi(2)
+        th(3)
+        hi(3)
+        bias_ps = psum.tile([P, O], F32, tag="bank", name="bias_ps")
+        nc.tensor.matmul(bias_ps[:], lhsT=ones[:], rhs=brow[:], start=True, stop=True)
+        nc.scalar.copy(out=biasB[:], in_=bias_ps[:])
+        tw("wff", wff_nat, 0)
+        cw("wff", wff_I, 0)
+        tw("wff", wff_nat, 1)
+        cw("wff", wff_I, 1)
+        st_a(0)
+        st_a(1)
+        quant_weight(w_I, w_codes, w_scales, 0)
+        quant_weight(w_I, w_codes, w_scales, 1)
+        st_b(0)
+        st_c(0)
+        st_c(1)
+        st_c(2)
+        st_c(3)
+        st_a(2)
+        st_d(0)
+        st_e(0)
+        st_f(0)
+        st_d(1)
+        st_e(1)
+        st_f(1)
+        st_a(3)
+        st_d(2)
+        st_e(2)
+        st_f(2)
+        st_d(3)
+        st_e(3)
+        st_f(3)
+        st_b(1)
+        st_c(4)
+        st_c(5)
+        st_c(6)
+        st_c(7)
+        quant_weight(wff_I, wff_codes, wff_scales, 0)
+        quant_weight(wff_I, wff_codes, wff_scales, 1)
+        st_g(0)
+        st_h(0)
+        st_h(1)
+        st_h(2)
+        st_h(3)
+        st_d(4)
+        st_e(4)
+        st_f(4)
+        st_d(5)
+        st_e(5)
+        st_f(5)
+        st_d(6)
+        st_e(6)
+        st_f(6)
+        st_d(7)
+        st_e(7)
+        st_f(7)
+        st_i(0)
+        st_j(0)
+        st_i(1)
+        st_j(1)
+        st_i(2)
+        st_j(2)
+        st_g(8)
+        st_h(4)
+        st_h(5)
+        st_i(3)
+        st_j(3)
+        st_g(9)
+        st_h(6)
+        st_h(7)
+        st_i(4)
+        st_j(4)
+        st_i(5)
+        st_j(5)
+        st_i(6)
+        st_j(6)
+        st_i(7, 0, 256)
+        st_j(7, 0, 256)
+        st_i(7, 256, 512)
+        st_j(7, 256, 512)

@@ -52,7 +52,8 @@ def tile_differ_amplifier_pa_kernel(tc, h, w, w_ff, b_ff, out):
 
         ones = const.tile([P, P], BF16, name="ones")
         nc.vector.memset(ones[:], 1.0)
-
+        junk = const.tile([P, O], BF16, name="junk")
+        nc.vector.memset(junk[:], 0.0)
         ident = const.tile([P, P], F32, name="ident")
         make_identity(nc, ident[:])
         brow = const.tile([P, O], BF16, name="brow")
@@ -62,6 +63,11 @@ def tile_differ_amplifier_pa_kernel(tc, h, w, w_ff, b_ff, out):
         nc.vector.memset(warm[:], 0.0)
         nc.scalar.activation(out=warm[:], in_=warm[:], func=ACT.Sigmoid)
 
+        warm_ps = psum.tile([P, O], F32, tag="bank", name="warm_ps")
+
+        def warm_up(count):
+            for rep in range(count):
+                nc.tensor.matmul(warm_ps[:], lhsT=ones[:], rhs=junk[:], start=True, stop=True)
 
         def transpose_words(bank, src_bf16):
             words = src_bf16.bitcast(F32)
@@ -226,6 +232,7 @@ def tile_differ_amplifier_pa_kernel(tc, h, w, w_ff, b_ff, out):
             nc.scalar.activation(out=res[i][:, lo:hi_], in_=pre[i][:, lo:hi_], func=ACT.Sigmoid)
             nc.sync.dma_start(out=out_v[:, i, lo:hi_], in_=res[i][:, lo:hi_])
 
+        warm_up(3)
         totals(0)
         th(0)
         hi(0)

from contextlib import ExitStack

import concourse.mybir as mybir
from concourse.masks import make_identity

N_ROWS, H, O = 1024, 512, 512
FLOPS = 2 * N_ROWS * H * H + 2 * N_ROWS * H * O

F32 = mybir.dt.float32
BF16 = mybir.dt.bfloat16
U32 = mybir.dt.uint32
U8 = mybir.dt.uint8
FP8X4 = mybir.dt.float8_e4m3fn_x4
ALU = mybir.AluOpType
ACT = mybir.ActivationFunctionType
AX = mybir.AxisListType

P = 128
NT = N_ROWS // P
BANK1 = F32


def tile_differ_amplifier_pa_kernel(tc, h, w, w_ff, b_ff, out):
    nc = tc.nc
    with ExitStack() as ctx:
        const = ctx.enter_context(tc.tile_pool(name="const", bufs=1))
        keep = ctx.enter_context(tc.tile_pool(name="keep", bufs=1))
        work = ctx.enter_context(tc.tile_pool(name="work", bufs=8))
        psum = ctx.enter_context(tc.psum_pool(name="psum", bufs=8))
        ctx.enter_context(tc.manual_schedule())

        h_v = h.rearrange("(p i) k -> p i k", i=NT)
        out_v = out.rearrange("(p i) o -> p i o", i=NT)
        w_v = w.rearrange("(j m) k -> m j k", j=4)
        wff_v = w_ff.rearrange("(j m) k -> m j k", j=4)

        h_nat = []
        for j in range(4):
            t = keep.tile([P, 2, H], BF16, name="h_nat%d" % j)
            nc.sync.dma_start(out=t[:], in_=h_v[:, 2 * j : 2 * j + 2, :])
            h_nat.append(t)
        w_nat = []
        for b in range(2):
            t = keep.tile([P, 2, H], BF16, name="w_nat%d" % b)
            nc.sync.dma_start(out=t[:], in_=w_v[:, 2 * b : 2 * b + 2, :])
            w_nat.append(t)
        wff_nat = []
        for b in range(2):
            t = keep.tile([P, 2, H], BF16, name="wff_nat%d" % b)
            nc.sync.dma_start(out=t[:], in_=wff_v[:, 2 * b : 2 * b + 2, :])
            wff_nat.append(t)

        ones = const.tile([P, P], BF16, name="ones")
        nc.vector.memset(ones[:], 1.0)
        junk = const.tile([P, O], BF16, name="junk")
        nc.vector.memset(junk[:], 0.0)
        ident = const.tile([P, P], F32, name="ident")
        make_identity(nc, ident[:])
        brow = const.tile([P, O], BF16, name="brow")
        nc.vector.memset(brow[:], 0.0)
        nc.scalar.dma_start(out=brow[0:1, :], in_=b_ff.rearrange("(a o) -> a o", a=1))
        warm = const.tile([P, 1], F32, name="warm")
        nc.vector.memset(warm[:], 0.0)
        nc.scalar.activation(out=warm[:], in_=warm[:], func=ACT.Sigmoid)

        warm_ps = psum.tile([P, O], F32, tag="bank", name="warm_ps")

        def warm_up(count):
            for rep in range(count):
                nc.tensor.matmul(warm_ps[:], lhsT=ones[:], rhs=junk[:], start=True, stop=True)

        def transpose_words(bank, src_bf16):
            words = src_bf16.bitcast(F32)
            for u in range(2):
                nc.tensor.transpose(bank[:, u, :], words[:, u : H // 2 : 2], ident[:])

        tot_ps = psum.tile([P, 4, NT], F32, tag="bank", name="tot_ps")
        hI = [None] * 4

        def totals(j):
            for ii in range(2):
                i = 2 * j + ii
                for t in range(4):
                    nc.tensor.matmul(
                        tot_ps[:, t, i : i + 1],
                        lhsT=h_nat[j][:, ii, t:H:4],
                        rhs=ones[:, 0:1],
                        start=True,
                        stop=True,
                    )

        tp_h = [None] * 4

        def th(j):
            tp_h[j] = psum.tile([P, 2, 2, P], F32, tag="bank", name="tp_h")
            for ii in range(2):
                transpose_words(tp_h[j][:, ii], h_nat[j][:, ii, :])

        def hi(j):
            hI[j] = keep.tile([P, 2 * P * 4], BF16, name="hI%d" % j, align_bytes=64)
            nc.scalar.copy(
                out=hI[j][:].bitcast(F32).rearrange("p (i n u) -> p i n u", i=2, u=2),
                in_=tp_h[j][:].rearrange("p i u n -> p i n u"),
            )

        def weight_tiles(label):
            grouped = keep.tile([P, O * 4], BF16, name=label + "_I", align_bytes=64)
            codes = keep.tile([P, O], U32, name=label + "_codes", align_bytes=64)
            scales = keep.tile([P, O], U8, name=label + "_scales", align_bytes=64)
            return grouped, codes, scales

        tp_w = {}

        def tw(label, nat, b):
            tp_w[(label, b)] = psum.tile([P, 2, 2, P], F32, tag="bank", name="tp_w")
            for jj in range(2):
                transpose_words(tp_w[(label, b)][:, jj], nat[b][:, jj, :])

        def cw(label, grouped, b):
            dst = grouped[:, b * 1024 : (b + 1) * 1024].bitcast(F32)
            nc.scalar.copy(
                out=dst.rearrange("p (j m u) -> p j m u", j=2, u=2),
                in_=tp_w[(label, b)][:].rearrange("p j u m -> p j m u"),
            )

        def quant_weight(grouped, codes, scales, b):
            nc.vector.quantize_mx(
                out=codes[:, b * 256 : (b + 1) * 256].bitcast(FP8X4),
                scales=scales[:, b * 256 : (b + 1) * 256],
                in_=grouped[:, b * 1024 : (b + 1) * 1024],
            )

        w_I, w_codes, w_scales = weight_tiles("w")
        wff_I, wff_codes, wff_scales = weight_tiles("wff")
        tot = const.tile([P, 4], F32, name="tot")
        cmean = const.tile([P, 4], F32, name="cmean")
        biasB = const.tile([P, O], F32, name="biasB")

        rI = []
        r_codes = []
        r_scales = []
        hnI = []
        hn_codes = []
        hn_scales = []
        for half in range(2):
            rI.append(keep.tile([P, 2048], BF16, name="rI%d" % half, align_bytes=64))
            r_codes.append(keep.tile([P, 512], U32, name="r_codes%d" % half, align_bytes=64))
            r_scales.append(keep.tile([P, 512], U8, name="r_scales%d" % half, align_bytes=64))
            hnI.append(keep.tile([P, 2048], BF16, name="hnI%d" % half, align_bytes=64))
            hn_codes.append(keep.tile([P, 512], U32, name="hn_codes%d" % half, align_bytes=64))
            hn_scales.append(keep.tile([P, 512], U8, name="hn_scales%d" % half, align_bytes=64))
        s1 = [None] * NT
        hn = [None] * NT
        tp_hn = [None] * NT
        s2 = [None] * NT
        pre = [None] * NT

        def st_a(j):
            nc.vector.scalar_tensor_tensor(
                out=rI[j // 2][:, (j % 2) * 1024 : (j % 2 + 1) * 1024].rearrange("p (n t) -> p n t", t=4),
                in0=hI[j][:].rearrange("p (n t) -> p n t", t=4),
                scalar=float(N_ROWS) / (N_ROWS - 1),
                in1=cmean[:].unsqueeze(1).to_broadcast([P, 2 * P, 4]),
                op0=ALU.mult,
                op1=ALU.subtract,
            )

        def st_b(half):
            nc.vector.quantize_mx(
                out=r_codes[half][:].bitcast(FP8X4), scales=r_scales[half][:], in_=rI[half][:]
            )

        def st_c(i):
            half, q = i // 4, i % 4
            s1[i] = psum.tile([P, H], BANK1, tag="bank", name="s1")
            nc.tensor.matmul_mx(
                out=s1[i][:],
                lhsT=r_codes[half][:, q * P : (q + 1) * P].bitcast(FP8X4),
                lhsT_scale=r_scales[half][:, q * P : (q + 1) * P],
                rhs=w_codes[:].bitcast(FP8X4),
                rhs_scale=w_scales[:],
                start=True,
                stop=True,
            )

        def st_d(i):
            hn[i] = work.tile([P, H], BF16, name="hn")
            nc.vector.tensor_tensor(out=hn[i][:], in0=s1[i][:], in1=h_nat[i // 2][:, i % 2, :], op=ALU.add)

        def st_e(i):
            tp_hn[i] = psum.tile([P, 2, P], F32, tag="bank", name="tp_hn")
            transpose_words(tp_hn[i], hn[i][:])

        def st_f(i):
            half, q = i // 4, i % 4
            nc.scalar.copy(
                out=hnI[half][:, q * 512 : (q + 1) * 512].bitcast(F32).rearrange("p (n u) -> p n u", u=2),
                in_=tp_hn[i][:].rearrange("p u n -> p n u"),
            )

        def st_g(part):
            half, lo, hi_ = {0: (0, 0, 4), 1: (1, 0, 4), 8: (1, 0, 2), 9: (1, 2, 4)}[part]
            nc.vector.quantize_mx(
                out=hn_codes[half][:, lo * P : hi_ * P].bitcast(FP8X4),
                scales=hn_scales[half][:, lo * P : hi_ * P],
                in_=hnI[half][:, lo * 4 * P : hi_ * 4 * P],
            )

        def st_h(i):
            half, q = i // 4, i % 4
            s2[i] = psum.tile([P, O], F32, tag="bank", name="s2")
            nc.tensor.matmul_mx(
                out=s2[i][:],
                lhsT=hn_codes[half][:, q * P : (q + 1) * P].bitcast(FP8X4),
                lhsT_scale=hn_scales[half][:, q * P : (q + 1) * P],
                rhs=wff_codes[:].bitcast(FP8X4),
                rhs_scale=wff_scales[:],
                start=True,
                stop=True,
            )

        res = [None] * NT

        def st_i(i, lo=0, hi_=O):
            if lo == 0:
                pre[i] = work.tile([P, O], F32, name="pre")
            nc.vector.tensor_tensor(out=pre[i][:, lo:hi_], in0=s2[i][:, lo:hi_], in1=biasB[:, lo:hi_], op=ALU.add)

        def st_j(i, lo=0, hi_=O):
            if lo == 0:
                res[i] = work.tile([P, O], F32, name="res")
            nc.scalar.activation(out=res[i][:, lo:hi_], in_=pre[i][:, lo:hi_], func=ACT.Sigmoid)
            nc.sync.dma_start(out=out_v[:, i, lo:hi_], in_=res[i][:, lo:hi_])

        warm_up(3)
        totals(0)
        th(0)
        hi(0)
        totals(1)
        totals(2)
        totals(3)
        nc.vector.tensor_reduce(out=tot[:], in_=tot_ps[:], axis=AX.X, op=ALU.add)
        nc.vector.tensor_scalar_mul(cmean[:], tot[:], 1.0 / (N_ROWS - 1))
        th(1)
        hi(1)
        tw("w", w_nat, 0)
        cw("w", w_I, 0)
        tw("w", w_nat, 1)
        cw("w", w_I, 1)
        th(2)
        hi(2)
        th(3)
        hi(3)
        bias_ps = psum.tile([P, O], F32, tag="bank", name="bias_ps")
        nc.tensor.matmul(bias_ps[:], lhsT=ones[:], rhs=brow[:], start=True, stop=True)
        nc.scalar.copy(out=biasB[:], in_=bias_ps[:])
        tw("wff", wff_nat, 0)
        cw("wff", wff_I, 0)
        tw("wff", wff_nat, 1)
        cw("wff", wff_I, 1)
        st_a(0)
        st_a(1)
        quant_weight(w_I, w_codes, w_scales, 0)
        quant_weight(w_I, w_codes, w_scales, 1)
        st_b(0)
        st_c(0)
        st_c(1)
        st_c(2)
        st_c(3)
        st_a(2)
        st_d(0)
        st_e(0)
        st_f(0)
        st_d(1)
        st_e(1)
        st_f(1)
        st_a(3)
        st_d(2)
        st_e(2)
        st_f(2)
        st_d(3)
        st_e(3)
        st_f(3)
        st_b(1)
        st_c(4)
        st_c(5)
        st_c(6)
        st_c(7)
        quant_weight(wff_I, wff_codes, wff_scales, 0)
        quant_weight(wff_I, wff_codes, wff_scales, 1)
        st_g(0)
        st_h(0)
        st_h(1)
        st_h(2)
        st_h(3)
        st_d(4)
        st_e(4)
        st_f(4)
        st_d(5)
        st_e(5)
        st_f(5)
        st_d(6)
        st_e(6)
        st_f(6)
        st_d(7)
        st_e(7)
        st_f(7)
        st_i(0)
        st_j(0)
        st_i(1)
        st_j(1)
        st_i(2)
        st_j(2)
        st_g(8)
        st_h(4)
        st_h(5)
        st_i(3)
        st_j(3)
        st_g(9)
        st_h(6)
        st_h(7)
        st_i(4)
        st_j(4)
        st_i(5)
        st_j(5)
        st_i(6)
        st_j(6)
        st_i(7, 0, 256)
        st_j(7, 0, 256)
        st_i(7, 256, 512)
        st_j(7, 256, 512)
